import numpy as np
import ml_dtypes


BF16 = ml_dtypes.bfloat16


def bf(x):
    return np.asarray(x, np.float32).astype(BF16)


def f64(x):
    return np.asarray(x).astype(np.float64)


E2M1 = np.array([0.0, 0.5, 1.0, 1.5, 2.0, 3.0, 4.0, 6.0, -0.0, -0.5, -1.0, -1.5, -2.0, -3.0, -4.0, -6.0])


def pack_weight(w, fmt):
    k, n = w.shape
    w = f64(bf(w)).reshape(k // 32, 32, n)
    amax = np.abs(w).max(1)
    if fmt == "e4m3":
        byte = np.frexp(amax)[1] - 1 + 127 - 7
    else:
        mant, ex = np.frexp(amax / 6.0)
        byte = np.where(mant > 0.5, ex, ex - 1) + 127
    byte = np.clip(np.where(amax > 0, byte, 1), 1, 254)
    scaled = (w * np.exp2(127.0 - byte)[:, None, :]).reshape(k, n).astype(np.float32)
    by_word = np.ascontiguousarray(scaled.reshape(k // 512, 128, 4, n).transpose(0, 1, 3, 2))
    if fmt == "e4m3":
        words = by_word.astype(ml_dtypes.float8_e4m3fn).view(np.uint8)
    else:
        c = by_word.astype(ml_dtypes.float4_e2m1fn).view(np.uint8) & 0xF
        words = c[..., 0::2] | (c[..., 1::2] << 4)
    return np.ascontiguousarray(words), np.ascontiguousarray(byte.astype(np.uint8).reshape(k // 512, 16, n))


def unpack_weight(words, scales, fmt):
    g, p, n, _ = words.shape
    if fmt == "e4m3":
        vals = np.ascontiguousarray(words).view(ml_dtypes.float8_e4m3fn).astype(np.float64)
    else:
        nib = np.empty((g, p, n, 4), np.uint8)
        nib[..., 0::2] = words & 0xF
        nib[..., 1::2] = words >> 4
        vals = E2M1[nib]
    vals = vals * np.repeat(np.exp2(scales.astype(np.float64) - 127.0), 8, axis=1)[..., None]
    return vals.transpose(0, 1, 3, 2).reshape(g * 512, n)

def pack4(w):
    words, scales = pack_weight(w, "e2m1")
    return words.reshape(words.shape[0], 128, -1), scales


def unpack4(words, scales):
    return unpack_weight(words.reshape(words.shape[0], 128, -1, 2), scales, "e2m1")


def kspread(k):
    return np.exp2(np.repeat(np.random.randint(-6, 7, k // 32), 32).astype(np.float64))


B, F, H, C = 1024, 3072, 512, 10
EPS = 4.0 / 30.0
P_KEEP = 0.95


def setup_inputs():
    s1 = kspread(F)
    s2 = kspread(F)
    ns = EPS / (6.0 * np.sqrt(H))
    x1 = np.random.standard_normal((B, F)) * s1
    x1_words, x1_scales = pack4(x1.reshape(B, F).T)
    x2 = np.random.standard_normal((B, F)) * s2
    x2_words, x2_scales = pack4(x2.reshape(B, F).T)
    W1_words, W1_scales = pack4(np.random.standard_normal((F, H)) / np.sqrt(F) / s1[:, None])
    b1 = bf(np.random.standard_normal(H) * 0.3)
    W2_words, W2_scales = pack4(np.random.standard_normal((F, H)) / np.sqrt(F) / s2[:, None])
    b2 = bf(np.random.standard_normal(H) * 0.3)
    noise_std = bf(np.random.laplace(size=(B, H)) * ns)
    rr_uniform = bf(np.random.uniform(size=H))
    return {"x1_words": x1_words,
            "x1_scales": x1_scales,
            "x2_words": x2_words,
            "x2_scales": x2_scales,
            "W1_words": W1_words,
            "W1_scales": W1_scales,
            "b1": b1,
            "W2_words": W2_words,
            "W2_scales": W2_scales,
            "b2": b2,
            "noise_std": noise_std,
            "rr_uniform": rr_uniform}


def reference(x1_words, x1_scales, x2_words, x2_scales, W1_words, W1_scales, b1, W2_words, W2_scales, b2, noise_std, rr_uniform):
    out1 = (unpack4(x1_words, x1_scales).T @ unpack4(W1_words, W1_scales)) + f64(b1)
    one_norm = np.sum(np.abs(out1), axis=1)
    sensitivity = np.max(one_norm) - np.min(one_norm)
    noise_mul = sensitivity / EPS
    out1 = out1 + f64(noise_std) * noise_mul
    rr_mask = np.where(f64(rr_uniform) < P_KEEP, 1.0, 0.0)
    out1 = out1 * rr_mask
    out2 = (unpack4(x2_words, x2_scales).T @ unpack4(W2_words, W2_scales)) + f64(b2)
    return np.minimum(out1, out2)

@@ -1,0 +1,279 @@
+from contextlib import ExitStack
+
+import concourse.mybir as mybir
+from concourse.masks import make_identity
+
+F32 = mybir.dt.float32
+BF16 = mybir.dt.bfloat16
+I32 = mybir.dt.int32
+U8 = mybir.dt.uint8
+FP4X4 = mybir.dt.float4_e2m1fn_x4
+ALU = mybir.AluOpType
+ACT = mybir.ActivationFunctionType
+AX = mybir.AxisListType
+
+P = 128
+ROWS, K, H = 1024, 3072, 512
+PASSES = K // 512
+BLOCKS = ROWS // P
+HALF = ROWS // 2
+KEEP_BELOW = 0.95
+INV_EPS = 7.5
+
+FLOPS = 2 * 2 * ROWS * K * H
+
+
+def tile_splitnn_pa_kernel(
+    tc, x1_words, x1_scales, x2_words, x2_scales, W1_words, W1_scales, b1,
+    W2_words, W2_scales, b2, noise_std, rr_uniform, out,
+):
+    nc = tc.nc
+    with ExitStack() as ctx:
+        keep_pool = ctx.enter_context(tc.tile_pool(name="keep", bufs=1))
+        psum = ctx.enter_context(tc.psum_pool(name="psum", bufs=1))
+        ctx.enter_context(tc.manual_schedule())
+
+        def sb(name, shape, dtype):
+            return keep_pool.tile(shape, dtype, name=name, align_bytes=256)
+
+        def bank(i):
+            return psum.tile([P, H], F32, name="bank%d" % i)
+
+        w1c = sb("w1c", [P, PASSES, 2 * H], U8)
+        w2c = sb("w2c", [P, PASSES, 2 * H], U8)
+        x1c = [sb("x1c%d" % h, [P, PASSES, 2 * HALF], U8) for h in range(2)]
+        x2c = sb("x2c", [P, PASSES, 2 * ROWS], U8)
+        w1s = sb("w1s", [P, PASSES, H], U8)
+        x1s = [sb("x1s%d" % h, [P, PASSES, HALF], U8) for h in range(2)]
+        w2s = sb("w2s", [P, PASSES, H], U8)
+        x2s = sb("x2s", [P, PASSES, ROWS], U8)
+        vec = sb("vec", [P, 3, H], BF16)
+        ones = sb("ones", [P, H], BF16)
+        noise = sb("noise", [P, BLOCKS, H], BF16)
+        b1_all = sb("b1_all", [P, H], F32)
+        b2_all = sb("b2_all", [P, H], F32)
+        keep_all = sb("keep_all", [P, H], BF16)
+        shift = sb("shift", [P, H], F32)
+        ident = sb("ident", [P, P], F32)
+        warm = sb("warm", [P, 1], F32)
+        l1 = sb("l1", [P, 2, BLOCKS], F32)
+        l1_rest = sb("l1_rest", [P, 1], F32)
+        ext = sb("ext", [P, 2], F32)
+        ext_all = sb("ext_all", [P, 2], F32)
+        mul = sb("mul", [P, 1], F32)
+        junk = sb("junk", [P, H], F32)
+        a = sb("a", [P, BLOCKS, H], F32)
+        nk = sb("nk", [P, BLOCKS, H], BF16)
+        ak = sb("ak", [P, BLOCKS, H], F32)
+        cc = sb("cc", [P, BLOCKS, H], F32)
+        dd = sb("dd", [P, BLOCKS, H], F32)
+        res = sb("res", [P, BLOCKS, H], F32)
+
+        nc.vector.memset(w1s[:].bitcast(I32), 0)
+        nc.vector.memset(x1s[0][:].bitcast(I32), 0)
+        nc.vector.memset(ones[:], 1.0)
+        nc.vector.memset(warm[:], 0.0)
+        nc.vector.memset(x1s[1][:].bitcast(I32), 0)
+        nc.gpsimd.memset(vec[:], 0.0)
+        nc.gpsimd.dma_start(out=vec[0:1, 0, :], in_=b1.unsqueeze(0))
+        nc.gpsimd.dma_start(out=vec[0:1, 2, :], in_=rr_uniform.unsqueeze(0))
+        nc.gpsimd.dma_start(out=vec[0:1, 1, :], in_=b2.unsqueeze(0))
+        nc.gpsimd.memset(w2s[:].bitcast(I32), 0)
+        nc.gpsimd.memset(x2s[:].bitcast(I32), 0)
+        make_identity(nc, ident[:])
+        nc.scalar.activation(out=warm[:], in_=warm[:], func=ACT.Abs)
+
+        def load_codes(dst, words, g0, g1, c0, c1):
+            nc.sync.dma_start(
+                out=dst[:, g0:g1, :].bitcast(I32),
+                in_=words[g0:g1, :, c0:c1].rearrange("g p n -> p g n").bitcast(I32),
+            )
+
+        def load_scales(dst, scales, c0, c1):
+            for q in range(4):
+                nc.sync.dma_start(
+                    out=dst[32 * q : 32 * q + 4, :, :].bitcast(I32),
+                    in_=scales[:, 4 * q : 4 * q + 4, c0:c1].rearrange("g r n -> r g n").bitcast(I32),
+                )
+
+        def load_noise(m0, m1):
+            nc.sync.dma_start(
+                out=noise[:, m0:m1, :],
+                in_=noise_std[P * m0 : P * m1, :].rearrange("(m p) c -> p m c", p=P),
+            )
+
+        load_codes(w1c, W1_words, 0, 1, 0, 2 * H)
+        load_codes(x1c[0], x1_words, 0, 1, 0, 2 * HALF)
+        load_scales(w1s, W1_scales, 0, H)
+        load_scales(x1s[0], x1_scales, 0, HALF)
+        load_codes(w1c, W1_words, 1, 2, 0, 2 * H)
+        load_codes(x1c[0], x1_words, 1, 2, 0, 2 * HALF)
+        load_codes(w1c, W1_words, 2, 3, 0, 2 * H)
+        load_codes(x1c[0], x1_words, 2, 3, 0, 2 * HALF)
+        load_codes(w1c, W1_words, 3, 6, 0, 2 * H)
+        load_codes(x1c[0], x1_words, 3, 6, 0, 2 * HALF)
+        load_scales(x1s[1], x1_scales, HALF, ROWS)
+        load_codes(x1c[1], x1_words, 0, 6, 2 * HALF, 4 * HALF)
+        load_noise(0, 4)
+        load_noise(4, 8)
+        load_codes(w2c, W2_words, 0, 6, 0, 2 * H)
+        load_scales(w2s, W2_scales, 0, H)
+        load_scales(x2s, x2_scales, 0, ROWS)
+        load_codes(x2c, x2_words, 0, 3, 0, 2 * ROWS)
+        load_codes(x2c, x2_words, 3, 6, 0, 2 * ROWS)
+
+        def pass1(acc, m, g, c0=0, c1=H):
+            h, mm = divmod(m, 4)
+            nc.tensor.matmul_mx(
+                out=acc[:, c0:c1],
+                lhsT=x1c[h][:, g, 256 * mm : 256 * mm + 256].bitcast(FP4X4),
+                lhsT_scale=x1s[h][:, g, P * mm : P * mm + P],
+                rhs=w1c[:, g, 2 * c0 : 2 * c1].bitcast(FP4X4),
+                rhs_scale=w1s[:, g, c0:c1],
+                start=(g == 0),
+                stop=(g == PASSES - 1),
+            )
+
+        def pass2(acc, m, g, c0=0, c1=H):
+            nc.tensor.matmul_mx(
+                out=acc[:, c0:c1],
+                lhsT=x2c[:, g, 256 * m : 256 * m + 256].bitcast(FP4X4),
+                lhsT_scale=x2s[:, g, P * m : P * m + P],
+                rhs=w2c[:, g, 2 * c0 : 2 * c1].bitcast(FP4X4),
+                rhs_scale=w2s[:, g, c0:c1],
+                start=(g == 0),
+                stop=(g == PASSES - 1),
+            )
+
+        acc1 = {}
+        acc2 = {}
+
+        def add_bias(m, c0=0, c1=H):
+            nc.vector.tensor_tensor(out=a[:, m, c0:c1], in0=acc1[m][:, c0:c1], in1=b1_all[:, c0:c1], op=ALU.add)
+
+        def norm(m, dst, c0=0, c1=H):
+            nc.scalar.activation(out=junk[:, c0:c1], in_=a[:, m, c0:c1], func=ACT.Abs, accum_out=dst)
+
+        def shifted_mask(m):
+            nc.vector.tensor_tensor(out=ak[:, m, :], in0=acc1[m][:], in1=keep_all[:], op=ALU.mult)
+            nc.gpsimd.tensor_tensor(out=ak[:, m, :], in0=ak[:, m, :], in1=shift[:], op=ALU.add)
+
+        def mask(eng, m):
+            eng.tensor_tensor(out=ak[:, m, :], in0=a[:, m, :], in1=keep_all[:], op=ALU.mult)
+
+        def masked_noise(m):
+            nc.vector.tensor_tensor(out=nk[:, m, :], in0=noise[:, m, :], in1=keep_all[:], op=ALU.mult)
+
+        FIRST = 3
+        warm_bank = bank(7)
+        for i in range(5):
+            nc.tensor.matmul(warm_bank[:], lhsT=ones[:, :P], rhs=ones[:], start=True, stop=True)
+        for m in range(FIRST):
+            acc1[m] = bank(m)
+        spread = {}
+        for g in range(PASSES):
+            for m in range(FIRST):
+                pass1(acc1[m], m, g)
+            if g == 3:
+                for i, v in ((4, 0), (5, 2), (6, 1)):
+                    spread[v] = bank(i)
+                    nc.tensor.matmul(spread[v][:], lhsT=ones[:, :P], rhs=vec[:, v, :], start=True, stop=True)
+        nc.scalar.copy(out=b1_all[:], in_=spread[0][:])
+        nc.vector.tensor_scalar(out=keep_all[:], in0=spread[2][:], scalar1=KEEP_BELOW, scalar2=None, op0=ALU.is_lt)
+        nc.scalar.copy(out=b2_all[:], in_=spread[1][:])
+        nc.vector.tensor_tensor(out=shift[:], in0=b1_all[:], in1=keep_all[:], op=ALU.mult)
+        nc.vector.tensor_tensor(out=shift[:], in0=shift[:], in1=b2_all[:], op=ALU.subtract)
+
+        SHIFTED = (1, 2, 3, 4)
+        for m in range(FIRST):
+            add_bias(m)
+            norm(m, l1[:, 0, m : m + 1])
+        shifted_mask(1)
+        shifted_mask(2)
+        mask(nc.gpsimd, 0)
+        for m in range(FIRST, 7):
+            acc1[m] = bank(m)
+            for g in range(PASSES):
+                pass1(acc1[m], m, g)
+            masked_noise(2 * (m - FIRST))
+            masked_noise(2 * (m - FIRST) + 1)
+            add_bias(m)
+            norm(m, l1[:, 0, m : m + 1])
+            if m in SHIFTED:
+                shifted_mask(m)
+            else:
+                mask(nc.gpsimd, m)
+        acc1[7] = bank(0)
+        for c0 in (0, 256):
+            for g in range(PASSES):
+                pass1(acc1[7], 7, g, c0, c0 + 256)
+        add_bias(7, 0, 256)
+        norm(7, l1[:, 0, 7:8], 0, 256)
+        add_bias(7, 256, 512)
+        norm(7, l1_rest[:], 256, 512)
+        mask(nc.vector, 7)
+        nc.vector.tensor_tensor(out=l1[:, 0, 7:8], in0=l1[:, 0, 7:8], in1=l1_rest[:], op=ALU.add)
+        nc.vector.tensor_scalar(out=l1[:, 1, :], in0=l1[:, 0, :], scalar1=-1.0, scalar2=None, op0=ALU.mult)
+        nc.vector.tensor_reduce(out=ext[:], in_=l1[:], axis=AX.X, op=ALU.max)
+
+        acc2[0] = bank(1)
+        for g in range(PASSES):
+            pass2(acc2[0], 0, g)
+            if g == 4:
+                spread_ext = bank(7)
+                for j in range(2):
+                    nc.tensor.transpose(
+                        spread_ext[:, P * j : P * j + P], ext[:, j : j + 1].to_broadcast([P, P]), ident[:]
+                    )
+        nc.vector.tensor_reduce(
+            out=ext_all[:], in_=spread_ext[:, 0 : 2 * P].rearrange("p (j n) -> p j n", j=2), axis=AX.X, op=ALU.max
+        )
+        nc.vector.tensor_scalar(
+            out=mul[:], in0=ext_all[:, 0:1], scalar1=ext_all[:, 1:2], scalar2=INV_EPS, op0=ALU.add, op1=ALU.mult
+        )
+        TAIL = [(0, 256), (256, 384), (384, 512)]
+        for m in range(1, BLOCKS):
+            acc2[m] = bank(m + 1 if m < 6 else (0, 7)[m - 6])
+            for c0, c1 in [(0, H)] if m < 7 else TAIL:
+                for g in range(PASSES):
+                    pass2(acc2[m], m, g, c0, c1)
+
+        def noisy(m0, m1):
+            nc.vector.scalar_tensor_tensor(
+                out=cc[:, m0:m1, :], in0=nk[:, m0:m1, :], scalar=mul[:], in1=ak[:, m0:m1, :], op0=ALU.mult, op1=ALU.add
+            )
+
+        def store(m, c0, c1):
+            nc.sync.dma_start(out=out[P * m : P * m + P, c0:c1], in_=res[:, m, c0:c1])
+
+        def other(m, c0=0, c1=H):
+            nc.vector.tensor_tensor(out=dd[:, m, c0:c1], in0=acc2[m][:, c0:c1], in1=b2_all[:, c0:c1], op=ALU.add)
+
+        def lower(m, c0=0, c1=H):
+            nc.vector.tensor_tensor(out=res[:, m, c0:c1], in0=dd[:, m, c0:c1], in1=cc[:, m, c0:c1], op=ALU.min)
+            store(m, c0, c1)
+
+        def lower_shifted(m):
+            nc.vector.tensor_tensor(out=dd[:, m, :], in0=acc2[m][:], in1=cc[:, m, :], op=ALU.min)
+            nc.gpsimd.tensor_tensor(out=res[:, m, :], in0=dd[:, m, :], in1=b2_all[:], op=ALU.add)
+            store(m, 0, H)
+
+        other(0)
+        noisy(0, 1)
+        lower(0)
+        noisy(1, 3)
+        lower_shifted(1)
+        lower_shifted(2)
+        noisy(3, 4)
+        lower_shifted(3)
+        noisy(4, 5)
+        lower_shifted(4)
+        noisy(5, 7)
+        other(5)
+        lower(5)
+        noisy(7, 8)
+        other(6)
+        lower(6)
+        for c0, c1 in TAIL:
+            other(7, c0, c1)
+            lower(7, c0, c1)

@@ -115,11 +115,11 @@ def tile_splitnn_pa_kernel(
         load_scales(x1s[1], x1_scales, HALF, ROWS)
         load_codes(x1c[1], x1_words, 0, 6, 2 * HALF, 4 * HALF)
         load_noise(0, 4)
-        load_noise(4, 8)
         load_codes(w2c, W2_words, 0, 6, 0, 2 * H)
         load_scales(w2s, W2_scales, 0, H)
         load_scales(x2s, x2_scales, 0, ROWS)
         load_codes(x2c, x2_words, 0, 3, 0, 2 * ROWS)
+        load_noise(4, 8)
         load_codes(x2c, x2_words, 3, 6, 0, 2 * ROWS)
 
         def pass1(acc, m, g, c0=0, c1=H):
@@ -184,25 +184,28 @@ def tile_splitnn_pa_kernel(
         nc.vector.tensor_tensor(out=shift[:], in0=b1_all[:], in1=keep_all[:], op=ALU.mult)
         nc.vector.tensor_tensor(out=shift[:], in0=shift[:], in1=b2_all[:], op=ALU.subtract)
 
-        SHIFTED = (1, 2, 3, 4)
+        SHIFTED = (0, 3)
         for m in range(FIRST):
             add_bias(m)
             norm(m, l1[:, 0, m : m + 1])
-        shifted_mask(1)
-        shifted_mask(2)
-        mask(nc.gpsimd, 0)
+        shifted_mask(0)
+        mask(nc.gpsimd, 1)
+        mask(nc.gpsimd, 2)
         for m in range(FIRST, 7):
             acc1[m] = bank(m)
             for g in range(PASSES):
                 pass1(acc1[m], m, g)
-            masked_noise(2 * (m - FIRST))
-            masked_noise(2 * (m - FIRST) + 1)
+            if m in (4, 5):
+                masked_noise(2 * (m - 4))
+                masked_noise(2 * (m - 4) + 1)
             add_bias(m)
             norm(m, l1[:, 0, m : m + 1])
             if m in SHIFTED:
                 shifted_mask(m)
-            else:
-                mask(nc.gpsimd, m)
+            elif m < 6:
+                mask(nc.vector, m)
+        masked_noise(4)
+        masked_noise(5)
         acc1[7] = bank(0)
         for c0 in (0, 256):
             for g in range(PASSES):
@@ -211,7 +214,8 @@ def tile_splitnn_pa_kernel(
         norm(7, l1[:, 0, 7:8], 0, 256)
         add_bias(7, 256, 512)
         norm(7, l1_rest[:], 256, 512)
-        mask(nc.vector, 7)
+        masked_noise(6)
+        masked_noise(7)
         nc.vector.tensor_tensor(out=l1[:, 0, 7:8], in0=l1[:, 0, 7:8], in1=l1_rest[:], op=ALU.add)
         nc.vector.tensor_scalar(out=l1[:, 1, :], in0=l1[:, 0, :], scalar1=-1.0, scalar2=None, op0=ALU.mult)
         nc.vector.tensor_reduce(out=ext[:], in_=l1[:], axis=AX.X, op=ALU.max)
@@ -225,18 +229,17 @@ def tile_splitnn_pa_kernel(
                     nc.tensor.transpose(
                         spread_ext[:, P * j : P * j + P], ext[:, j : j + 1].to_broadcast([P, P]), ident[:]
                     )
+        mask(nc.vector, 6)
         nc.vector.tensor_reduce(
             out=ext_all[:], in_=spread_ext[:, 0 : 2 * P].rearrange("p (j n) -> p j n", j=2), axis=AX.X, op=ALU.max
         )
         nc.vector.tensor_scalar(
             out=mul[:], in0=ext_all[:, 0:1], scalar1=ext_all[:, 1:2], scalar2=INV_EPS, op0=ALU.add, op1=ALU.mult
         )
-        TAIL = [(0, 256), (256, 384), (384, 512)]
         for m in range(1, BLOCKS):
             acc2[m] = bank(m + 1 if m < 6 else (0, 7)[m - 6])
-            for c0, c1 in [(0, H)] if m < 7 else TAIL:
-                for g in range(PASSES):
-                    pass2(acc2[m], m, g, c0, c1)
+            for g in range(PASSES):
+                pass2(acc2[m], m, g)
 
         def noisy(m0, m1):
             nc.vector.scalar_tensor_tensor(
@@ -249,31 +252,30 @@ def tile_splitnn_pa_kernel(
         def other(m, c0=0, c1=H):
             nc.vector.tensor_tensor(out=dd[:, m, c0:c1], in0=acc2[m][:, c0:c1], in1=b2_all[:, c0:c1], op=ALU.add)
 
-        def lower(m, c0=0, c1=H):
-            nc.vector.tensor_tensor(out=res[:, m, c0:c1], in0=dd[:, m, c0:c1], in1=cc[:, m, c0:c1], op=ALU.min)
-            store(m, c0, c1)
+        def lower(m0, m1, c0=0, c1=H):
+            nc.vector.tensor_tensor(out=res[:, m0:m1, c0:c1], in0=dd[:, m0:m1, c0:c1], in1=cc[:, m0:m1, c0:c1], op=ALU.min)
+            for m in range(m0, m1):
+                store(m, c0, c1)
 
         def lower_shifted(m):
             nc.vector.tensor_tensor(out=dd[:, m, :], in0=acc2[m][:], in1=cc[:, m, :], op=ALU.min)
             nc.gpsimd.tensor_tensor(out=res[:, m, :], in0=dd[:, m, :], in1=b2_all[:], op=ALU.add)
             store(m, 0, H)
 
-        other(0)
-        noisy(0, 1)
-        lower(0)
-        noisy(1, 3)
-        lower_shifted(1)
-        lower_shifted(2)
-        noisy(3, 4)
+        noisy(0, 3)
+        lower_shifted(0)
+        other(1)
+        other(2)
+        lower(1, 3)
+        noisy(3, 6)
         lower_shifted(3)
-        noisy(4, 5)
-        lower_shifted(4)
-        noisy(5, 7)
+        other(4)
         other(5)
-        lower(5)
-        noisy(7, 8)
+        lower(4, 6)
+        mask(nc.vector, 7)
+        noisy(6, 8)
         other(6)
-        lower(6)
-        for c0, c1 in TAIL:
-            other(7, c0, c1)
-            lower(7, c0, c1)
+        lower(6, 7)
+        other(7)
+        lower(7, 8, 0, 256)
+        lower(7, 8, 256, 512)

@@ -53,7 +53,8 @@ def tile_splitnn_pa_kernel(
         b1_all = sb("b1_all", [P, H], F32)
         b2_all = sb("b2_all", [P, H], F32)
         keep_all = sb("keep_all", [P, H], BF16)
-        shift = sb("shift", [P, H], F32)
+        b2_col = sb("b2_col", [P, 8], F32)
+        dT = sb("dT", [P, 4, H], F32)
         ident = sb("ident", [P, P], F32)
         warm = sb("warm", [P, 1], F32)
         l1 = sb("l1", [P, 2, BLOCKS], F32)
@@ -74,13 +75,13 @@ def tile_splitnn_pa_kernel(
         nc.vector.memset(ones[:], 1.0)
         nc.vector.memset(warm[:], 0.0)
         nc.vector.memset(x1s[1][:].bitcast(I32), 0)
-        nc.gpsimd.memset(vec[:], 0.0)
-        nc.gpsimd.dma_start(out=vec[0:1, 0, :], in_=b1.unsqueeze(0))
+        nc.gpsimd.memset(vec[:].rearrange("p v c -> p (v c)").bitcast(I32), 0)
         nc.gpsimd.dma_start(out=vec[0:1, 2, :], in_=rr_uniform.unsqueeze(0))
+        nc.gpsimd.dma_start(out=vec[0:1, 0, :], in_=b1.unsqueeze(0))
         nc.gpsimd.dma_start(out=vec[0:1, 1, :], in_=b2.unsqueeze(0))
+        make_identity(nc, ident[:])
         nc.gpsimd.memset(w2s[:].bitcast(I32), 0)
         nc.gpsimd.memset(x2s[:].bitcast(I32), 0)
-        make_identity(nc, ident[:])
         nc.scalar.activation(out=warm[:], in_=warm[:], func=ACT.Abs)
 
         def load_codes(dst, words, g0, g1, c0, c1):
@@ -90,10 +91,10 @@ def tile_splitnn_pa_kernel(
             )
 
         def load_scales(dst, scales, c0, c1):
-            for q in range(4):
+            for r in range(4):
                 nc.sync.dma_start(
-                    out=dst[32 * q : 32 * q + 4, :, :].bitcast(I32),
-                    in_=scales[:, 4 * q : 4 * q + 4, c0:c1].rearrange("g r n -> r g n").bitcast(I32),
+                    out=dst[r:P:32, :, :].bitcast(I32),
+                    in_=scales[:, r:16:4, c0:c1].rearrange("g q n -> q g n").bitcast(I32),
                 )
 
         def load_noise(m0, m1):
@@ -104,17 +105,17 @@ def tile_splitnn_pa_kernel(
 
         load_codes(w1c, W1_words, 0, 1, 0, 2 * H)
         load_codes(x1c[0], x1_words, 0, 1, 0, 2 * HALF)
-        load_scales(w1s, W1_scales, 0, H)
-        load_scales(x1s[0], x1_scales, 0, HALF)
         load_codes(w1c, W1_words, 1, 2, 0, 2 * H)
         load_codes(x1c[0], x1_words, 1, 2, 0, 2 * HALF)
+        load_scales(w1s, W1_scales, 0, H)
+        load_scales(x1s[0], x1_scales, 0, HALF)
         load_codes(w1c, W1_words, 2, 3, 0, 2 * H)
         load_codes(x1c[0], x1_words, 2, 3, 0, 2 * HALF)
         load_codes(w1c, W1_words, 3, 6, 0, 2 * H)
         load_codes(x1c[0], x1_words, 3, 6, 0, 2 * HALF)
+        load_noise(0, 4)
         load_scales(x1s[1], x1_scales, HALF, ROWS)
         load_codes(x1c[1], x1_words, 0, 6, 2 * HALF, 4 * HALF)
-        load_noise(0, 4)
         load_codes(w2c, W2_words, 0, 6, 0, 2 * H)
         load_scales(w2s, W2_scales, 0, H)
         load_scales(x2s, x2_scales, 0, ROWS)
@@ -154,10 +155,6 @@ def tile_splitnn_pa_kernel(
         def norm(m, dst, c0=0, c1=H):
             nc.scalar.activation(out=junk[:, c0:c1], in_=a[:, m, c0:c1], func=ACT.Abs, accum_out=dst)
 
-        def shifted_mask(m):
-            nc.vector.tensor_tensor(out=ak[:, m, :], in0=acc1[m][:], in1=keep_all[:], op=ALU.mult)
-            nc.gpsimd.tensor_tensor(out=ak[:, m, :], in0=ak[:, m, :], in1=shift[:], op=ALU.add)
-
         def mask(eng, m):
             eng.tensor_tensor(out=ak[:, m, :], in0=a[:, m, :], in1=keep_all[:], op=ALU.mult)
 
@@ -166,7 +163,7 @@ def tile_splitnn_pa_kernel(
 
         FIRST = 3
         warm_bank = bank(7)
-        for i in range(5):
+        for i in range(6):
             nc.tensor.matmul(warm_bank[:], lhsT=ones[:, :P], rhs=ones[:], start=True, stop=True)
         for m in range(FIRST):
             acc1[m] = bank(m)
@@ -174,38 +171,41 @@ def tile_splitnn_pa_kernel(
         for g in range(PASSES):
             for m in range(FIRST):
                 pass1(acc1[m], m, g)
-            if g == 3:
-                for i, v in ((4, 0), (5, 2), (6, 1)):
+            if g == 4:
+                for i, v in ((4, 2), (5, 0), (6, 1)):
                     spread[v] = bank(i)
                     nc.tensor.matmul(spread[v][:], lhsT=ones[:, :P], rhs=vec[:, v, :], start=True, stop=True)
+                col_bank = bank(7)
+                for j in range(4):
+                    nc.tensor.matmul(
+                        col_bank[:, 2 * j : 2 * j + 2], lhsT=vec[:, 1, P * j : P * j + P], rhs=ones[:, 0:2], start=True, stop=True
+                    )
         nc.scalar.copy(out=b1_all[:], in_=spread[0][:])
         nc.vector.tensor_scalar(out=keep_all[:], in0=spread[2][:], scalar1=KEEP_BELOW, scalar2=None, op0=ALU.is_lt)
         nc.scalar.copy(out=b2_all[:], in_=spread[1][:])
-        nc.vector.tensor_tensor(out=shift[:], in0=b1_all[:], in1=keep_all[:], op=ALU.mult)
-        nc.vector.tensor_tensor(out=shift[:], in0=shift[:], in1=b2_all[:], op=ALU.subtract)
+        nc.scalar.copy(out=b2_col[:], in_=col_bank[:, 0:8])
+        for m in range(4):
+            masked_noise(m)
 
-        SHIFTED = (0, 3)
         for m in range(FIRST):
             add_bias(m)
             norm(m, l1[:, 0, m : m + 1])
-        shifted_mask(0)
+        mask(nc.gpsimd, 0)
         mask(nc.gpsimd, 1)
         mask(nc.gpsimd, 2)
         for m in range(FIRST, 7):
             acc1[m] = bank(m)
             for g in range(PASSES):
                 pass1(acc1[m], m, g)
-            if m in (4, 5):
-                masked_noise(2 * (m - 4))
-                masked_noise(2 * (m - 4) + 1)
+            if m == 5:
+                masked_noise(4)
+                masked_noise(5)
             add_bias(m)
             norm(m, l1[:, 0, m : m + 1])
-            if m in SHIFTED:
-                shifted_mask(m)
-            elif m < 6:
-                mask(nc.vector, m)
-        masked_noise(4)
-        masked_noise(5)
+            if m < 6:
+                mask(nc.gpsimd, m)
+        masked_noise(6)
+        masked_noise(7)
         acc1[7] = bank(0)
         for c0 in (0, 256):
             for g in range(PASSES):
@@ -214,21 +214,30 @@ def tile_splitnn_pa_kernel(
         norm(7, l1[:, 0, 7:8], 0, 256)
         add_bias(7, 256, 512)
         norm(7, l1_rest[:], 256, 512)
-        masked_noise(6)
-        masked_noise(7)
+        mask(nc.vector, 7)
         nc.vector.tensor_tensor(out=l1[:, 0, 7:8], in0=l1[:, 0, 7:8], in1=l1_rest[:], op=ALU.add)
         nc.vector.tensor_scalar(out=l1[:, 1, :], in0=l1[:, 0, :], scalar1=-1.0, scalar2=None, op0=ALU.mult)
         nc.vector.tensor_reduce(out=ext[:], in_=l1[:], axis=AX.X, op=ALU.max)
 
-        acc2[0] = bank(1)
-        for g in range(PASSES):
-            pass2(acc2[0], 0, g)
-            if g == 4:
-                spread_ext = bank(7)
-                for j in range(2):
-                    nc.tensor.transpose(
-                        spread_ext[:, P * j : P * j + P], ext[:, j : j + 1].to_broadcast([P, P]), ident[:]
-                    )
+        for j in range(4):
+            accT = bank(j + 1)
+            for g in range(PASSES):
+                nc.tensor.matmul_mx(
+                    out=accT[:],
+                    lhsT=w2c[:, g, 256 * j : 256 * j + 256].bitcast(FP4X4),
+                    lhsT_scale=w2s[:, g, P * j : P * j + P],
+                    rhs=x2c[:, g, 0 : 2 * HALF].bitcast(FP4X4),
+                    rhs_scale=x2s[:, g, 0:HALF],
+                    start=(g == 0),
+                    stop=(g == PASSES - 1),
+                )
+                if j == 0 and g == 5:
+                    spread_ext = bank(7)
+                    for i in range(2):
+                        nc.tensor.transpose(
+                            spread_ext[:, P * i : P * i + P], ext[:, i : i + 1].to_broadcast([P, P]), ident[:]
+                        )
+            nc.scalar.activation(out=dT[:, j, :], in_=accT[:], func=ACT.Identity, bias=b2_col[:, 2 * j : 2 * j + 1])
         mask(nc.vector, 6)
         nc.vector.tensor_reduce(
             out=ext_all[:], in_=spread_ext[:, 0 : 2 * P].rearrange("p (j n) -> p j n", j=2), axis=AX.X, op=ALU.max
@@ -236,46 +245,49 @@ def tile_splitnn_pa_kernel(
         nc.vector.tensor_scalar(
             out=mul[:], in0=ext_all[:, 0:1], scalar1=ext_all[:, 1:2], scalar2=INV_EPS, op0=ALU.add, op1=ALU.mult
         )
-        for m in range(1, BLOCKS):
-            acc2[m] = bank(m + 1 if m < 6 else (0, 7)[m - 6])
-            for g in range(PASSES):
-                pass2(acc2[m], m, g)
+
+        def direct(m, i, cuts=((0, H),)):
+            acc2[m] = bank(i)
+            for c0, c1 in cuts:
+                for g in range(PASSES):
+                    pass2(acc2[m], m, g, c0, c1)
+
+        direct(4, 5)
+        for m, i in ((0, 6), (1, 0), (2, 1), (3, 2)):
+            acc2[m] = bank(i)
+            for j in range(4):
+                nc.tensor.transpose(acc2[m][:, P * j : P * j + P], dT[:, j, P * m : P * m + P], ident[:])
+        direct(5, 3)
+        direct(6, 4)
+        direct(7, 7, ((0, 256), (256, 512)))
 
         def noisy(m0, m1):
             nc.vector.scalar_tensor_tensor(
                 out=cc[:, m0:m1, :], in0=nk[:, m0:m1, :], scalar=mul[:], in1=ak[:, m0:m1, :], op0=ALU.mult, op1=ALU.add
             )
 
-        def store(m, c0, c1):
+        def store(m, c0=0, c1=H):
             nc.sync.dma_start(out=out[P * m : P * m + P, c0:c1], in_=res[:, m, c0:c1])
 
         def other(m, c0=0, c1=H):
             nc.vector.tensor_tensor(out=dd[:, m, c0:c1], in0=acc2[m][:, c0:c1], in1=b2_all[:, c0:c1], op=ALU.add)
 
-        def lower(m0, m1, c0=0, c1=H):
-            nc.vector.tensor_tensor(out=res[:, m0:m1, c0:c1], in0=dd[:, m0:m1, c0:c1], in1=cc[:, m0:m1, c0:c1], op=ALU.min)
-            for m in range(m0, m1):
-                store(m, c0, c1)
+        def lower(m, c0=0, c1=H):
+            nc.vector.tensor_tensor(out=res[:, m, c0:c1], in0=dd[:, m, c0:c1], in1=cc[:, m, c0:c1], op=ALU.min)
+            store(m, c0, c1)
 
-        def lower_shifted(m):
-            nc.vector.tensor_tensor(out=dd[:, m, :], in0=acc2[m][:], in1=cc[:, m, :], op=ALU.min)
-            nc.gpsimd.tensor_tensor(out=res[:, m, :], in0=dd[:, m, :], in1=b2_all[:], op=ALU.add)
-            store(m, 0, H)
-
-        noisy(0, 3)
-        lower_shifted(0)
-        other(1)
-        other(2)
-        lower(1, 3)
-        noisy(3, 6)
-        lower_shifted(3)
-        other(4)
-        other(5)
-        lower(4, 6)
-        mask(nc.vector, 7)
+        noisy(0, 2)
+        noisy(2, 4)
+        noisy(4, 6)
         noisy(6, 8)
-        other(6)
-        lower(6, 7)
-        other(7)
-        lower(7, 8, 0, 256)
-        lower(7, 8, 256, 512)
+        other(4)
+        lower(4)
+        for m in range(4):
+            nc.vector.tensor_tensor(out=res[:, m, :], in0=acc2[m][:], in1=cc[:, m, :], op=ALU.min)
+            store(m)
+        for m in (5, 6):
+            other(m)
+            lower(m)
+        for c0, c1 in ((0, 256), (256, 512)):
+            other(7, c0, c1)
+            lower(7, c0, c1)

@@ -42,11 +42,11 @@ def tile_splitnn_pa_kernel(
         w1c = sb("w1c", [P, PASSES, 2 * H], U8)
         w2c = sb("w2c", [P, PASSES, 2 * H], U8)
         x1c = [sb("x1c%d" % h, [P, PASSES, 2 * HALF], U8) for h in range(2)]
-        x2c = sb("x2c", [P, PASSES, 2 * ROWS], U8)
+        x2c = [sb("x2c%d" % h, [P, PASSES, 2 * HALF], U8) for h in range(2)]
         w1s = sb("w1s", [P, PASSES, H], U8)
         x1s = [sb("x1s%d" % h, [P, PASSES, HALF], U8) for h in range(2)]
         w2s = sb("w2s", [P, PASSES, H], U8)
-        x2s = sb("x2s", [P, PASSES, ROWS], U8)
+        x2s = [sb("x2s%d" % h, [P, PASSES, HALF], U8) for h in range(2)]
         vec = sb("vec", [P, 3, H], BF16)
         ones = sb("ones", [P, H], BF16)
         noise = sb("noise", [P, BLOCKS, H], BF16)
@@ -57,7 +57,7 @@ def tile_splitnn_pa_kernel(
         dT = sb("dT", [P, 4, H], F32)
         ident = sb("ident", [P, P], F32)
         warm = sb("warm", [P, 1], F32)
-        l1 = sb("l1", [P, 2, BLOCKS], F32)
+        l1 = sb("l1", [P, BLOCKS], F32)
         l1_rest = sb("l1_rest", [P, 1], F32)
         ext = sb("ext", [P, 2], F32)
         ext_all = sb("ext_all", [P, 2], F32)
@@ -81,7 +81,8 @@ def tile_splitnn_pa_kernel(
         nc.gpsimd.dma_start(out=vec[0:1, 1, :], in_=b2.unsqueeze(0))
         make_identity(nc, ident[:])
         nc.gpsimd.memset(w2s[:].bitcast(I32), 0)
-        nc.gpsimd.memset(x2s[:].bitcast(I32), 0)
+        nc.gpsimd.memset(x2s[0][:].bitcast(I32), 0)
+        nc.gpsimd.memset(x2s[1][:].bitcast(I32), 0)
         nc.scalar.activation(out=warm[:], in_=warm[:], func=ACT.Abs)
 
         def load_codes(dst, words, g0, g1, c0, c1):
@@ -105,23 +106,25 @@ def tile_splitnn_pa_kernel(
 
         load_codes(w1c, W1_words, 0, 1, 0, 2 * H)
         load_codes(x1c[0], x1_words, 0, 1, 0, 2 * HALF)
-        load_codes(w1c, W1_words, 1, 2, 0, 2 * H)
-        load_codes(x1c[0], x1_words, 1, 2, 0, 2 * HALF)
         load_scales(w1s, W1_scales, 0, H)
         load_scales(x1s[0], x1_scales, 0, HALF)
+        load_codes(w1c, W1_words, 1, 2, 0, 2 * H)
+        load_codes(x1c[0], x1_words, 1, 2, 0, 2 * HALF)
         load_codes(w1c, W1_words, 2, 3, 0, 2 * H)
         load_codes(x1c[0], x1_words, 2, 3, 0, 2 * HALF)
         load_codes(w1c, W1_words, 3, 6, 0, 2 * H)
         load_codes(x1c[0], x1_words, 3, 6, 0, 2 * HALF)
         load_noise(0, 4)
+        load_noise(4, 8)
         load_scales(x1s[1], x1_scales, HALF, ROWS)
-        load_codes(x1c[1], x1_words, 0, 6, 2 * HALF, 4 * HALF)
+        load_codes(x1c[1], x1_words, 0, 3, 2 * HALF, 4 * HALF)
+        load_codes(x1c[1], x1_words, 3, 6, 2 * HALF, 4 * HALF)
         load_codes(w2c, W2_words, 0, 6, 0, 2 * H)
         load_scales(w2s, W2_scales, 0, H)
-        load_scales(x2s, x2_scales, 0, ROWS)
-        load_codes(x2c, x2_words, 0, 3, 0, 2 * ROWS)
-        load_noise(4, 8)
-        load_codes(x2c, x2_words, 3, 6, 0, 2 * ROWS)
+        load_scales(x2s[0], x2_scales, 0, HALF)
+        load_codes(x2c[0], x2_words, 0, 6, 0, 2 * HALF)
+        load_scales(x2s[1], x2_scales, HALF, ROWS)
+        load_codes(x2c[1], x2_words, 0, 6, 2 * HALF, 4 * HALF)
 
         def pass1(acc, m, g, c0=0, c1=H):
             h, mm = divmod(m, 4)
@@ -138,8 +141,8 @@ def tile_splitnn_pa_kernel(
         def pass2(acc, m, g, c0=0, c1=H):
             nc.tensor.matmul_mx(
                 out=acc[:, c0:c1],
-                lhsT=x2c[:, g, 256 * m : 256 * m + 256].bitcast(FP4X4),
-                lhsT_scale=x2s[:, g, P * m : P * m + P],
+                lhsT=x2c[1][:, g, 256 * (m - 4) : 256 * (m - 3)].bitcast(FP4X4),
+                lhsT_scale=x2s[1][:, g, P * (m - 4) : P * (m - 3)],
                 rhs=w2c[:, g, 2 * c0 : 2 * c1].bitcast(FP4X4),
                 rhs_scale=w2s[:, g, c0:c1],
                 start=(g == 0),
@@ -163,61 +166,66 @@ def tile_splitnn_pa_kernel(
 
         FIRST = 3
         warm_bank = bank(7)
-        for i in range(6):
+        for i in range(5):
             nc.tensor.matmul(warm_bank[:], lhsT=ones[:, :P], rhs=ones[:], start=True, stop=True)
         for m in range(FIRST):
             acc1[m] = bank(m)
         spread = {}
+
+        def spread_vector(i, v):
+            spread[v] = bank(i)
+            nc.tensor.matmul(spread[v][:], lhsT=ones[:, :P], rhs=vec[:, v, :], start=True, stop=True)
+
         for g in range(PASSES):
             for m in range(FIRST):
                 pass1(acc1[m], m, g)
+            if g == 2:
+                spread_vector(4, 2)
+                spread_vector(5, 0)
             if g == 4:
-                for i, v in ((4, 2), (5, 0), (6, 1)):
-                    spread[v] = bank(i)
-                    nc.tensor.matmul(spread[v][:], lhsT=ones[:, :P], rhs=vec[:, v, :], start=True, stop=True)
+                spread_vector(6, 1)
                 col_bank = bank(7)
                 for j in range(4):
                     nc.tensor.matmul(
                         col_bank[:, 2 * j : 2 * j + 2], lhsT=vec[:, 1, P * j : P * j + P], rhs=ones[:, 0:2], start=True, stop=True
                     )
-        nc.scalar.copy(out=b1_all[:], in_=spread[0][:])
         nc.vector.tensor_scalar(out=keep_all[:], in0=spread[2][:], scalar1=KEEP_BELOW, scalar2=None, op0=ALU.is_lt)
+        nc.scalar.copy(out=b1_all[:], in_=spread[0][:])
         nc.scalar.copy(out=b2_all[:], in_=spread[1][:])
         nc.scalar.copy(out=b2_col[:], in_=col_bank[:, 0:8])
-        for m in range(4):
+        for m in range(BLOCKS):
             masked_noise(m)
 
-        for m in range(FIRST):
+        def sums(m):
             add_bias(m)
-            norm(m, l1[:, 0, m : m + 1])
-        mask(nc.gpsimd, 0)
-        mask(nc.gpsimd, 1)
-        mask(nc.gpsimd, 2)
+            norm(m, l1[:, m : m + 1])
+
         for m in range(FIRST, 7):
             acc1[m] = bank(m)
             for g in range(PASSES):
                 pass1(acc1[m], m, g)
-            if m == 5:
-                masked_noise(4)
-                masked_noise(5)
-            add_bias(m)
-            norm(m, l1[:, 0, m : m + 1])
-            if m < 6:
-                mask(nc.gpsimd, m)
-        masked_noise(6)
-        masked_noise(7)
+        for m in range(FIRST):
+            sums(m)
+            mask(nc.gpsimd, m)
+        sums(3)
+        sums(4)
+        sums(5)
+        mask(nc.vector, 3)
+        mask(nc.vector, 4)
+        sums(6)
+        mask(nc.vector, 5)
         acc1[7] = bank(0)
         for c0 in (0, 256):
             for g in range(PASSES):
                 pass1(acc1[7], 7, g, c0, c0 + 256)
         add_bias(7, 0, 256)
-        norm(7, l1[:, 0, 7:8], 0, 256)
+        norm(7, l1[:, 7:8], 0, 256)
         add_bias(7, 256, 512)
         norm(7, l1_rest[:], 256, 512)
-        mask(nc.vector, 7)
-        nc.vector.tensor_tensor(out=l1[:, 0, 7:8], in0=l1[:, 0, 7:8], in1=l1_rest[:], op=ALU.add)
-        nc.vector.tensor_scalar(out=l1[:, 1, :], in0=l1[:, 0, :], scalar1=-1.0, scalar2=None, op0=ALU.mult)
-        nc.vector.tensor_reduce(out=ext[:], in_=l1[:], axis=AX.X, op=ALU.max)
+        mask(nc.vector, 6)
+        nc.vector.tensor_scalar(out=l1[:, 7:8], in0=l1[:, 7:8], scalar1=l1_rest[:], scalar2=None, op0=ALU.add)
+        nc.vector.tensor_reduce(out=ext[:, 0:1], in_=l1[:], axis=AX.X, op=ALU.max)
+        nc.vector.tensor_reduce(out=ext[:, 1:2], in_=l1[:], axis=AX.X, op=ALU.min)
 
         for j in range(4):
             accT = bank(j + 1)
@@ -226,8 +234,8 @@ def tile_splitnn_pa_kernel(
                     out=accT[:],
                     lhsT=w2c[:, g, 256 * j : 256 * j + 256].bitcast(FP4X4),
                     lhsT_scale=w2s[:, g, P * j : P * j + P],
-                    rhs=x2c[:, g, 0 : 2 * HALF].bitcast(FP4X4),
-                    rhs_scale=x2s[:, g, 0:HALF],
+                    rhs=x2c[0][:, g, :].bitcast(FP4X4),
+                    rhs_scale=x2s[0][:, g, :],
                     start=(g == 0),
                     stop=(g == PASSES - 1),
                 )
@@ -238,12 +246,11 @@ def tile_splitnn_pa_kernel(
                             spread_ext[:, P * i : P * i + P], ext[:, i : i + 1].to_broadcast([P, P]), ident[:]
                         )
             nc.scalar.activation(out=dT[:, j, :], in_=accT[:], func=ACT.Identity, bias=b2_col[:, 2 * j : 2 * j + 1])
-        mask(nc.vector, 6)
-        nc.vector.tensor_reduce(
-            out=ext_all[:], in_=spread_ext[:, 0 : 2 * P].rearrange("p (j n) -> p j n", j=2), axis=AX.X, op=ALU.max
-        )
+        mask(nc.vector, 7)
+        nc.vector.tensor_reduce(out=ext_all[:, 0:1], in_=spread_ext[:, 0:P], axis=AX.X, op=ALU.max)
+        nc.vector.tensor_reduce(out=ext_all[:, 1:2], in_=spread_ext[:, P : 2 * P], axis=AX.X, op=ALU.min)
         nc.vector.tensor_scalar(
-            out=mul[:], in0=ext_all[:, 0:1], scalar1=ext_all[:, 1:2], scalar2=INV_EPS, op0=ALU.add, op1=ALU.mult
+            out=mul[:], in0=ext_all[:, 0:1], scalar1=ext_all[:, 1:2], scalar2=INV_EPS, op0=ALU.subtract, op1=ALU.mult
         )
 
         def direct(m, i, cuts=((0, H),)):
@@ -276,10 +283,8 @@ def tile_splitnn_pa_kernel(
             nc.vector.tensor_tensor(out=res[:, m, c0:c1], in0=dd[:, m, c0:c1], in1=cc[:, m, c0:c1], op=ALU.min)
             store(m, c0, c1)
 
-        noisy(0, 2)
-        noisy(2, 4)
-        noisy(4, 6)
-        noisy(6, 8)
+        noisy(0, 4)
+        noisy(4, 8)
         other(4)
         lower(4)
         for m in range(4):

from contextlib import ExitStack

import concourse.mybir as mybir
from concourse.masks import make_identity

F32 = mybir.dt.float32
BF16 = mybir.dt.bfloat16
I32 = mybir.dt.int32
U8 = mybir.dt.uint8
FP4X4 = mybir.dt.float4_e2m1fn_x4
ALU = mybir.AluOpType
ACT = mybir.ActivationFunctionType
AX = mybir.AxisListType

P = 128
ROWS, K, H = 1024, 3072, 512
PASSES = K // 512
BLOCKS = ROWS // P
HALF = ROWS // 2
KEEP_BELOW = 0.95
INV_EPS = 7.5

FLOPS = 2 * 2 * ROWS * K * H


def tile_splitnn_pa_kernel(
    tc, x1_words, x1_scales, x2_words, x2_scales, W1_words, W1_scales, b1,
    W2_words, W2_scales, b2, noise_std, rr_uniform, out,
):
    nc = tc.nc
    with ExitStack() as ctx:
        keep_pool = ctx.enter_context(tc.tile_pool(name="keep", bufs=1))
        psum = ctx.enter_context(tc.psum_pool(name="psum", bufs=1))
        ctx.enter_context(tc.manual_schedule())

        def sb(name, shape, dtype):
            return keep_pool.tile(shape, dtype, name=name, align_bytes=256)

        def bank(i):
            return psum.tile([P, H], F32, name="bank%d" % i)

        w1c = sb("w1c", [P, PASSES, 2 * H], U8)
        w2c = sb("w2c", [P, PASSES, 2 * H], U8)
        x1c = [sb("x1c%d" % h, [P, PASSES, 2 * HALF], U8) for h in range(2)]
        x2c = [sb("x2c%d" % h, [P, PASSES, 2 * HALF], U8) for h in range(2)]
        w1s = sb("w1s", [P, PASSES, H], U8)
        x1s = [sb("x1s%d" % h, [P, PASSES, HALF], U8) for h in range(2)]
        w2s = sb("w2s", [P, PASSES, H], U8)
        x2s = [sb("x2s%d" % h, [P, PASSES, HALF], U8) for h in range(2)]
        vec = sb("vec", [P, 3, H], BF16)
        ones = sb("ones", [P, H], BF16)
        noise = sb("noise", [P, BLOCKS, H], BF16)
        b1_all = sb("b1_all", [P, H], F32)
        b2_all = sb("b2_all", [P, H], F32)
        keep_all = sb("keep_all", [P, H], BF16)
        b2_col = sb("b2_col", [P, 8], F32)
        dT = sb("dT", [P, 4, H], F32)
        ident = sb("ident", [P, P], F32)
        warm = sb("warm", [P, 1], F32)
        l1 = sb("l1", [P, BLOCKS], F32)
        l1_rest = sb("l1_rest", [P, 1], F32)
        ext = sb("ext", [P, 2], F32)
        ext_all = sb("ext_all", [P, 2], F32)
        mul = sb("mul", [P, 1], F32)
        junk = sb("junk", [P, H], F32)
        a = sb("a", [P, BLOCKS, H], F32)
        nk = sb("nk", [P, BLOCKS, H], BF16)
        ak = sb("ak", [P, BLOCKS, H], F32)
        cc = sb("cc", [P, BLOCKS, H], F32)
        dd = sb("dd", [P, BLOCKS, H], F32)
        res = sb("res", [P, BLOCKS, H], F32)

        nc.vector.memset(w1s[:].bitcast(I32), 0)
        nc.vector.memset(x1s[0][:].bitcast(I32), 0)
        nc.vector.memset(ones[:], 1.0)
        nc.vector.memset(warm[:], 0.0)
        nc.vector.memset(x1s[1][:].bitcast(I32), 0)
        nc.gpsimd.memset(vec[:].rearrange("p v c -> p (v c)").bitcast(I32), 0)
        nc.gpsimd.dma_start(out=vec[0:1, 2, :], in_=rr_uniform.unsqueeze(0))
        nc.gpsimd.dma_start(out=vec[0:1, 0, :], in_=b1.unsqueeze(0))
        nc.gpsimd.dma_start(out=vec[0:1, 1, :], in_=b2.unsqueeze(0))
        make_identity(nc, ident[:])
        nc.gpsimd.memset(w2s[:].bitcast(I32), 0)
        nc.gpsimd.memset(x2s[0][:].bitcast(I32), 0)
        nc.gpsimd.memset(x2s[1][:].bitcast(I32), 0)
        nc.scalar.activation(out=warm[:], in_=warm[:], func=ACT.Abs)

        def load_codes(dst, words, g0, g1, c0, c1):
            nc.sync.dma_start(
                out=dst[:, g0:g1, :].bitcast(I32),
                in_=words[g0:g1, :, c0:c1].rearrange("g p n -> p g n").bitcast(I32),
            )

        def load_scales(dst, scales, c0, c1):
            for r in range(4):
                nc.sync.dma_start(
                    out=dst[r:P:32, :, :].bitcast(I32),
                    in_=scales[:, r:16:4, c0:c1].rearrange("g q n -> q g n").bitcast(I32),
                )

        def load_noise(m0, m1):
            nc.sync.dma_start(
                out=noise[:, m0:m1, :],
                in_=noise_std[P * m0 : P * m1, :].rearrange("(m p) c -> p m c", p=P),
            )

        load_codes(w1c, W1_words, 0, 1, 0, 2 * H)
        load_codes(x1c[0], x1_words, 0, 1, 0, 2 * HALF)
        load_scales(w1s, W1_scales, 0, H)
        load_scales(x1s[0], x1_scales, 0, HALF)
        load_codes(w1c, W1_words, 1, 2, 0, 2 * H)
        load_codes(x1c[0], x1_words, 1, 2, 0, 2 * HALF)
        load_codes(w1c, W1_words, 2, 3, 0, 2 * H)
        load_codes(x1c[0], x1_words, 2, 3, 0, 2 * HALF)
        load_codes(w1c, W1_words, 3, 6, 0, 2 * H)
        load_codes(x1c[0], x1_words, 3, 6, 0, 2 * HALF)
        load_noise(0, 4)
        load_noise(4, 8)
        load_scales(x1s[1], x1_scales, HALF, ROWS)
        load_codes(x1c[1], x1_words, 0, 3, 2 * HALF, 4 * HALF)
        load_codes(x1c[1], x1_words, 3, 6, 2 * HALF, 4 * HALF)
        load_codes(w2c, W2_words, 0, 6, 0, 2 * H)
        load_scales(w2s, W2_scales, 0, H)
        load_scales(x2s[0], x2_scales, 0, HALF)
        load_codes(x2c[0], x2_words, 0, 6, 0, 2 * HALF)
        load_scales(x2s[1], x2_scales, HALF, ROWS)
        load_codes(x2c[1], x2_words, 0, 6, 2 * HALF, 4 * HALF)

        def pass1(acc, m, g, c0=0, c1=H):
            h, mm = divmod(m, 4)
            nc.tensor.matmul_mx(
                out=acc[:, c0:c1],
                lhsT=x1c[h][:, g, 256 * mm : 256 * mm + 256].bitcast(FP4X4),
                lhsT_scale=x1s[h][:, g, P * mm : P * mm + P],
                rhs=w1c[:, g, 2 * c0 : 2 * c1].bitcast(FP4X4),
                rhs_scale=w1s[:, g, c0:c1],
                start=(g == 0),
                stop=(g == PASSES - 1),
            )

        def pass2(acc, m, g, c0=0, c1=H):
            nc.tensor.matmul_mx(
                out=acc[:, c0:c1],
                lhsT=x2c[1][:, g, 256 * (m - 4) : 256 * (m - 3)].bitcast(FP4X4),
                lhsT_scale=x2s[1][:, g, P * (m - 4) : P * (m - 3)],
                rhs=w2c[:, g, 2 * c0 : 2 * c1].bitcast(FP4X4),
                rhs_scale=w2s[:, g, c0:c1],
                start=(g == 0),
                stop=(g == PASSES - 1),
            )

        acc1 = {}
        acc2 = {}

        def add_bias(m, c0=0, c1=H):
            nc.vector.tensor_tensor(out=a[:, m, c0:c1], in0=acc1[m][:, c0:c1], in1=b1_all[:, c0:c1], op=ALU.add)

        def norm(m, dst, c0=0, c1=H):
            nc.scalar.activation(out=junk[:, c0:c1], in_=a[:, m, c0:c1], func=ACT.Abs, accum_out=dst)

        def mask(eng, m):
            eng.tensor_tensor(out=ak[:, m, :], in0=a[:, m, :], in1=keep_all[:], op=ALU.mult)

        def masked_noise(m):
            nc.vector.tensor_tensor(out=nk[:, m, :], in0=noise[:, m, :], in1=keep_all[:], op=ALU.mult)

        FIRST = 3
        warm_bank = bank(7)
        for i in range(5):
            nc.tensor.matmul(warm_bank[:], lhsT=ones[:, :P], rhs=ones[:], start=True, stop=True)
        for m in range(FIRST):
            acc1[m] = bank(m)
        spread = {}

        def spread_vector(i, v):
            spread[v] = bank(i)
            nc.tensor.matmul(spread[v][:], lhsT=ones[:, :P], rhs=vec[:, v, :], start=True, stop=True)

        for g in range(PASSES):
            for m in range(FIRST):
                pass1(acc1[m], m, g)
            if g == 2:
                spread_vector(4, 2)
                spread_vector(5, 0)
            if g == 4:
                spread_vector(6, 1)
                col_bank = bank(7)
                for j in range(4):
                    nc.tensor.matmul(
                        col_bank[:, 2 * j : 2 * j + 2], lhsT=vec[:, 1, P * j : P * j + P], rhs=ones[:, 0:2], start=True, stop=True
                    )
        nc.vector.tensor_scalar(out=keep_all[:], in0=spread[2][:], scalar1=KEEP_BELOW, scalar2=None, op0=ALU.is_lt)
        nc.scalar.copy(out=b1_all[:], in_=spread[0][:])
        nc.scalar.copy(out=b2_all[:], in_=spread[1][:])
        nc.scalar.copy(out=b2_col[:], in_=col_bank[:, 0:8])
        for m in range(BLOCKS):
            masked_noise(m)

        def sums(m):
            add_bias(m)
            norm(m, l1[:, m : m + 1])

        for m in range(FIRST, 7):
            acc1[m] = bank(m)
            for g in range(PASSES):
                pass1(acc1[m], m, g)
        for m in range(FIRST):
            sums(m)
            mask(nc.gpsimd, m)
        sums(3)
        sums(4)
        sums(5)
        mask(nc.vector, 3)
        mask(nc.vector, 4)
        sums(6)
        mask(nc.vector, 5)
        acc1[7] = bank(0)
        for c0 in (0, 256):
            for g in range(PASSES):
                pass1(acc1[7], 7, g, c0, c0 + 256)
        add_bias(7, 0, 256)
        norm(7, l1[:, 7:8], 0, 256)
        add_bias(7, 256, 512)
        norm(7, l1_rest[:], 256, 512)
        mask(nc.vector, 6)
        nc.vector.tensor_scalar(out=l1[:, 7:8], in0=l1[:, 7:8], scalar1=l1_rest[:], scalar2=None, op0=ALU.add)
        nc.vector.tensor_reduce(out=ext[:, 0:1], in_=l1[:], axis=AX.X, op=ALU.max)
        nc.vector.tensor_reduce(out=ext[:, 1:2], in_=l1[:], axis=AX.X, op=ALU.min)

        for j in range(4):
            accT = bank(j + 1)
            for g in range(PASSES):
                nc.tensor.matmul_mx(
                    out=accT[:],
                    lhsT=w2c[:, g, 256 * j : 256 * j + 256].bitcast(FP4X4),
                    lhsT_scale=w2s[:, g, P * j : P * j + P],
                    rhs=x2c[0][:, g, :].bitcast(FP4X4),
                    rhs_scale=x2s[0][:, g, :],
                    start=(g == 0),
                    stop=(g == PASSES - 1),
                )
                if j == 0 and g == 5:
                    spread_ext = bank(7)
                    for i in range(2):
                        nc.tensor.transpose(
                            spread_ext[:, P * i : P * i + P], ext[:, i : i + 1].to_broadcast([P, P]), ident[:]
                        )
            nc.scalar.activation(out=dT[:, j, :], in_=accT[:], func=ACT.Identity, bias=b2_col[:, 2 * j : 2 * j + 1])
        mask(nc.vector, 7)
        nc.vector.tensor_reduce(out=ext_all[:, 0:1], in_=spread_ext[:, 0:P], axis=AX.X, op=ALU.max)
        nc.vector.tensor_reduce(out=ext_all[:, 1:2], in_=spread_ext[:, P : 2 * P], axis=AX.X, op=ALU.min)
        nc.vector.tensor_scalar(
            out=mul[:], in0=ext_all[:, 0:1], scalar1=ext_all[:, 1:2], scalar2=INV_EPS, op0=ALU.subtract, op1=ALU.mult
        )

        def direct(m, i, cuts=((0, H),)):
            acc2[m] = bank(i)
            for c0, c1 in cuts:
                for g in range(PASSES):
                    pass2(acc2[m], m, g, c0, c1)

        direct(4, 5)
        for m, i in ((0, 6), (1, 0), (2, 1), (3, 2)):
            acc2[m] = bank(i)
            for j in range(4):
                nc.tensor.transpose(acc2[m][:, P * j : P * j + P], dT[:, j, P * m : P * m + P], ident[:])
        direct(5, 3)
        direct(6, 4)
        direct(7, 7, ((0, 256), (256, 512)))

        def noisy(m0, m1):
            nc.vector.scalar_tensor_tensor(
                out=cc[:, m0:m1, :], in0=nk[:, m0:m1, :], scalar=mul[:], in1=ak[:, m0:m1, :], op0=ALU.mult, op1=ALU.add
            )

        def store(m, c0=0, c1=H):
            nc.sync.dma_start(out=out[P * m : P * m + P, c0:c1], in_=res[:, m, c0:c1])

        def other(m, c0=0, c1=H):
            nc.vector.tensor_tensor(out=dd[:, m, c0:c1], in0=acc2[m][:, c0:c1], in1=b2_all[:, c0:c1], op=ALU.add)

        def lower(m, c0=0, c1=H):
            nc.vector.tensor_tensor(out=res[:, m, c0:c1], in0=dd[:, m, c0:c1], in1=cc[:, m, c0:c1], op=ALU.min)
            store(m, c0, c1)

        noisy(0, 4)
        noisy(4, 8)
        other(4)
        lower(4)
        for m in range(4):
            nc.vector.tensor_tensor(out=res[:, m, :], in0=acc2[m][:], in1=cc[:, m, :], op=ALU.min)
            store(m)
        for m in (5, 6):
            other(m)
            lower(m)
        for c0, c1 in ((0, 256), (256, 512)):
            other(7, c0, c1)
            lower(7, c0, c1)
